import numpy as np
import ml_dtypes


def mxq(x, axis, fmt="e4m3"):
    dtype, down = {"e4m3": (ml_dtypes.float8_e4m3fn, 7), "e5m2": (ml_dtypes.float8_e5m2, 14)}[fmt]
    v = np.moveaxis(np.asarray(x, np.float32).astype(ml_dtypes.bfloat16).astype(np.float64), axis, -1)
    blocks = v.reshape(v.shape[:-1] + (-1, 32))
    amax = np.abs(blocks).max(-1, keepdims=True)
    byte = np.maximum(np.where(amax > 0, np.frexp(amax)[1] - 1 + 127, 0) - down, 1)
    scale = np.exp2(byte - 127.0)
    codes = (blocks / scale).astype(np.float32).astype(dtype).astype(np.float64)
    return np.moveaxis((codes * scale).reshape(v.shape), -1, axis)


WIDE = False


def mx_kscale(k):
    if not WIDE:
        return np.ones(k)
    levels = np.array([10, -10, 5, -5, 0])
    a = np.random.permutation(np.resize(levels, k // 512 * 4)).reshape(k // 512, 4)
    idx = np.arange(k)
    return np.exp2(a[idx // 512, idx % 128 // 32])


BF16 = ml_dtypes.bfloat16


def bf(x):
    return np.asarray(x, np.float32).astype(BF16)


def f64(x):
    return np.asarray(x).astype(np.float64)


B, N, D, H = 1, 512, 512, 512
EDGE_P = 0.01
DEG = 1.0 + EDGE_P * N


def normalize_adj(adj):
    rowsum = adj.sum(axis=1)
    d_inv_sqrt = np.where(rowsum > 0, 1.0 / np.sqrt(np.maximum(rowsum, 1e-30)), 0.0)
    return d_inv_sqrt[:, :, None] * adj.transpose(0, 2, 1) * d_inv_sqrt[:, None, :]


def setup_inputs():
    t = mx_kscale(H)
    adj = (np.random.uniform(size=(B, N, N)) < EDGE_P).astype(np.float64)
    adj = np.minimum(adj + np.eye(N)[None], 1.0)
    return {"msg": bf(np.random.standard_normal((B, N, H)) * 0.5 * np.sqrt(DEG) * t),
            "adj": bf(adj),
            "b2": bf(np.random.standard_normal(H) * 0.2 * t),
            "W3": bf(np.random.standard_normal((H, D)) * 0.5 * np.sqrt(DEG / H) / t[:, None])}


def reference(msg, adj, b2, W3):
    a = normalize_adj(f64(adj))
    h = np.maximum((mxq(a, 2, "e4m3") @ mxq(f64(msg), 1, "e4m3")) + f64(b2), 0.0)
    return mxq(h, 2, "e4m3") @ mxq(f64(W3), 0, "e4m3")

@@ -1,0 +1,173 @@
+from contextlib import ExitStack
+
+import concourse.mybir as mybir
+from concourse.masks import make_identity
+
+F32 = mybir.dt.float32
+BF16 = mybir.dt.bfloat16
+U32 = mybir.dt.uint32
+U8 = mybir.dt.uint8
+FP8X4 = mybir.dt.float8_e4m3fn_x4
+ALU = mybir.AluOpType
+ACT = mybir.ActivationFunctionType
+
+P = 128
+PACK = 4
+NODES = 512
+HIDDEN = 512
+DOUT = 512
+CHUNK = 128
+CHUNKS = NODES // CHUNK
+ONES_COLS = 32
+D_MAX = 1e15
+
+FLOPS = 2 * NODES * NODES * HIDDEN + 2 * NODES * HIDDEN * DOUT
+
+
+def load_k_first(nc, pool, name, rows):
+    planes = pool.tile([P, PACK, rows.shape[1]], BF16, name=name)
+    nc.sync.dma_start(out=planes[:], in_=rows.rearrange("(q p) w -> p q w", p=P))
+    return planes
+
+
+def regroup(nc, grouped, planes):
+    nc.vector.tensor_copy(
+        out=grouped.rearrange("p (c i) q -> p c q i", i=4),
+        in_=planes.rearrange("p q (c i) -> p c q i", i=4),
+    )
+
+
+def quantise(nc, pool, name, grouped):
+    width = grouped.shape[1]
+    codes = pool.tile([P, width], U32, name=name + "_codes", align_bytes=64)
+    scales = pool.tile([P, width], U8, name=name + "_scales", align_bytes=64)
+    nc.vector.quantize_mx(
+        out=codes[:].bitcast(FP8X4),
+        scales=scales[:],
+        in_=grouped.rearrange("p w q -> p (w q)"),
+    )
+    return codes, scales
+
+
+def tile_perception_pb_s_kernel(tc, msg, adj, b2, W3, out):
+    nc = tc.nc
+    with ExitStack() as ctx:
+        keep = ctx.enter_context(tc.tile_pool(name="keep", bufs=1))
+        work = ctx.enter_context(tc.tile_pool(name="work", bufs=CHUNKS))
+        ps_head = ctx.enter_context(tc.psum_pool(name="ps_head", bufs=1))
+        ps_h = ctx.enter_context(tc.psum_pool(name="ps_h", bufs=CHUNKS))
+        ps_o = ctx.enter_context(tc.psum_pool(name="ps_o", bufs=2))
+
+        adj_sb = load_k_first(nc, keep, "adj_sb", adj[0])
+        msg_sb = load_k_first(nc, keep, "msg_sb", msg[0])
+        w3_sb = load_k_first(nc, keep, "w3_sb", W3)
+
+        ident_f = keep.tile([P, P], F32)
+        make_identity(nc, ident_f[:])
+        ident_b = keep.tile([P, P], BF16)
+        make_identity(nc, ident_b[:])
+        ones = keep.tile([P, ONES_COLS], BF16)
+        nc.vector.memset(ones[:], 1.0)
+        one_col = keep.tile([P, 1], F32)
+        nc.vector.memset(one_col[:], 1.0)
+        table_warm = keep.tile([P, 1], F32)
+        nc.scalar.activation(out=table_warm[:], in_=one_col[:], func=ACT.Abs_reciprocal_sqrt)
+
+        b2_rows = keep.tile([P, P], BF16)
+        nc.vector.memset(b2_rows[:], 0.0)
+        nc.scalar.dma_start(out=b2_rows[0:PACK, :], in_=b2.rearrange("(q p) -> q p", p=P))
+        b2_ps = ps_head.tile([P, P], BF16, tag="early")
+        nc.tensor.transpose(b2_ps[:], b2_rows[:], ident_b[:])
+        b2_col = keep.tile([P, PACK], F32)
+        nc.vector.tensor_copy(out=b2_col[:], in_=b2_ps[:, 0:PACK])
+
+        c_ps = ps_head.tile([P, PACK, ONES_COLS], F32, tag="early")
+        for t in range(PACK):
+            for q in range(PACK):
+                nc.tensor.matmul(
+                    out=c_ps[:, t, :],
+                    lhsT=adj_sb[:, q, t * P : (t + 1) * P],
+                    rhs=ones[:],
+                    start=(q == 0),
+                    stop=(q == PACK - 1),
+                )
+        c_col = c_ps[:, :, 0]
+
+        rsqrt_c = keep.tile([P, PACK], F32)
+        nc.scalar.activation(out=rsqrt_c[:], in_=c_col, func=ACT.Abs_reciprocal_sqrt)
+        rsqrt_cap = keep.tile([P, PACK], F32)
+        nc.vector.tensor_scalar_min(out=rsqrt_cap[:], in0=rsqrt_c[:], scalar1=D_MAX)
+        d_rep = keep.tile([P, PACK, P], F32)
+        nc.vector.scalar_tensor_tensor(
+            out=d_rep[:],
+            in0=c_col.unsqueeze(2).to_broadcast([P, PACK, P]),
+            scalar=0.0,
+            in1=rsqrt_cap[:].unsqueeze(2).to_broadcast([P, PACK, P]),
+            op0=ALU.is_gt,
+            op1=ALU.mult,
+        )
+        d_row = ps_head.tile([P, PACK, P], F32)
+        for t in range(PACK):
+            nc.tensor.transpose(d_row[:, t, :], d_rep[:, t, :], ident_f[:])
+
+        msg_grp = keep.tile([P, HIDDEN, PACK], BF16, align_bytes=64)
+        regroup(nc, msg_grp[:], msg_sb[:])
+        msg_codes, msg_scales = quantise(nc, keep, "msg", msg_grp[:])
+
+        h_banks = []
+        for t in range(CHUNKS):
+            cols = slice(t * CHUNK, (t + 1) * CHUNK)
+            adj_dj = work.tile([P, PACK, CHUNK], F32)
+            for q in range(PACK):
+                nc.scalar.activation(
+                    out=adj_dj[:, q, :], in_=adj_sb[:, q, cols], func=ACT.Copy, scale=d_rep[:, q, 0:1]
+                )
+            a_grp = work.tile([P, CHUNK, PACK], BF16, align_bytes=64)
+            nc.vector.tensor_tensor(
+                out=a_grp[:],
+                in0=adj_dj[:].rearrange("p q c -> p c q"),
+                in1=d_row[:, t, :].unsqueeze(2).to_broadcast([P, CHUNK, PACK]),
+                op=ALU.mult,
+            )
+            a_codes, a_scales = quantise(nc, work, "a", a_grp[:])
+            h_ps = ps_h.tile([P, PACK, CHUNK], F32)
+            for q in range(PACK):
+                f_cols = slice(q * P, (q + 1) * P)
+                nc.tensor.matmul_mx(
+                    out=h_ps[:, q, :],
+                    lhsT=msg_codes[:, f_cols].bitcast(FP8X4),
+                    lhsT_scale=msg_scales[:, f_cols],
+                    rhs=a_codes[:].bitcast(FP8X4),
+                    rhs_scale=a_scales[:],
+                    start=True,
+                    stop=True,
+                )
+            h_banks.append(h_ps)
+            if t == 1:
+                w3_grp = keep.tile([P, DOUT, PACK], BF16, align_bytes=64)
+                regroup(nc, w3_grp[:], w3_sb[:])
+                w3_codes, w3_scales = quantise(nc, keep, "w3", w3_grp[:])
+
+        for t in range(CHUNKS):
+            h_ps = h_banks[t]
+            h_planes = work.tile([P, PACK, CHUNK], BF16)
+            for q in range(PACK):
+                nc.scalar.activation(
+                    out=h_planes[:, q, :], in_=h_ps[:, q, :], func=ACT.Relu, bias=b2_col[:, q : q + 1]
+                )
+            h_grp = work.tile([P, CHUNK, PACK], BF16, align_bytes=64)
+            regroup(nc, h_grp[:], h_planes[:])
+            h_codes, h_scales = quantise(nc, work, "h", h_grp[:])
+            o_ps = ps_o.tile([P, DOUT], F32)
+            nc.tensor.matmul_mx(
+                out=o_ps[:],
+                lhsT=h_codes[:].bitcast(FP8X4),
+                lhsT_scale=h_scales[:],
+                rhs=w3_codes[:].bitcast(FP8X4),
+                rhs_scale=w3_scales[:],
+                start=True,
+                stop=True,
+            )
+            o_sb = work.tile([P, DOUT], F32)
+            nc.scalar.copy(out=o_sb[:], in_=o_ps[:])
+            nc.sync.dma_start(out=out[0, t * CHUNK : (t + 1) * CHUNK, :], in_=o_sb[:])

@@ -18,6 +18,7 @@ HIDDEN = 512
 DOUT = 512
 CHUNK = 128
 CHUNKS = NODES // CHUNK
+PLANES_PER_BANK = 512 // CHUNK
 ONES_COLS = 32
 D_MAX = 1e15
 
@@ -30,11 +31,13 @@ def load_k_first(nc, pool, name, rows):
     return planes
 
 
-def regroup(nc, grouped, planes):
+def regroup(nc, pool, name, planes):
+    grouped = pool.tile([P, planes.shape[2], PACK], BF16, name=name, align_bytes=64)
     nc.vector.tensor_copy(
-        out=grouped.rearrange("p (c i) q -> p c q i", i=4),
+        out=grouped[:].rearrange("p (c i) q -> p c q i", i=4),
         in_=planes.rearrange("p q (c i) -> p c q i", i=4),
     )
+    return grouped
 
 
 def quantise(nc, pool, name, grouped):
@@ -44,7 +47,7 @@ def quantise(nc, pool, name, grouped):
     nc.vector.quantize_mx(
         out=codes[:].bitcast(FP8X4),
         scales=scales[:],
-        in_=grouped.rearrange("p w q -> p (w q)"),
+        in_=grouped[:].rearrange("p w q -> p (w q)"),
     )
     return codes, scales
 
@@ -52,15 +55,17 @@ def quantise(nc, pool, name, grouped):
 def tile_perception_pb_s_kernel(tc, msg, adj, b2, W3, out):
     nc = tc.nc
     with ExitStack() as ctx:
+        ctx.enter_context(tc.manual_schedule())
         keep = ctx.enter_context(tc.tile_pool(name="keep", bufs=1))
         work = ctx.enter_context(tc.tile_pool(name="work", bufs=CHUNKS))
-        ps_head = ctx.enter_context(tc.psum_pool(name="ps_head", bufs=1))
-        ps_h = ctx.enter_context(tc.psum_pool(name="ps_h", bufs=CHUNKS))
-        ps_o = ctx.enter_context(tc.psum_pool(name="ps_o", bufs=2))
+        psum = ctx.enter_context(tc.psum_pool(name="psum", bufs=4))
 
         adj_sb = load_k_first(nc, keep, "adj_sb", adj[0])
         msg_sb = load_k_first(nc, keep, "msg_sb", msg[0])
         w3_sb = load_k_first(nc, keep, "w3_sb", W3)
+        b2_rows = keep.tile([P, P], BF16)
+        nc.vector.memset(b2_rows[:], 0.0)
+        nc.scalar.dma_start(out=b2_rows[0:PACK, :], in_=b2.rearrange("(q p) -> q p", p=P))
 
         ident_f = keep.tile([P, P], F32)
         make_identity(nc, ident_f[:])
@@ -73,15 +78,7 @@ def tile_perception_pb_s_kernel(tc, msg, adj, b2, W3, out):
         table_warm = keep.tile([P, 1], F32)
         nc.scalar.activation(out=table_warm[:], in_=one_col[:], func=ACT.Abs_reciprocal_sqrt)
 
-        b2_rows = keep.tile([P, P], BF16)
-        nc.vector.memset(b2_rows[:], 0.0)
-        nc.scalar.dma_start(out=b2_rows[0:PACK, :], in_=b2.rearrange("(q p) -> q p", p=P))
-        b2_ps = ps_head.tile([P, P], BF16, tag="early")
-        nc.tensor.transpose(b2_ps[:], b2_rows[:], ident_b[:])
-        b2_col = keep.tile([P, PACK], F32)
-        nc.vector.tensor_copy(out=b2_col[:], in_=b2_ps[:, 0:PACK])
-
-        c_ps = ps_head.tile([P, PACK, ONES_COLS], F32, tag="early")
+        c_ps = psum.tile([P, PACK, ONES_COLS], F32, tag="rest")
         for t in range(PACK):
             for q in range(PACK):
                 nc.tensor.matmul(
@@ -97,77 +94,114 @@ def tile_perception_pb_s_kernel(tc, msg, adj, b2, W3, out):
         nc.scalar.activation(out=rsqrt_c[:], in_=c_col, func=ACT.Abs_reciprocal_sqrt)
         rsqrt_cap = keep.tile([P, PACK], F32)
         nc.vector.tensor_scalar_min(out=rsqrt_cap[:], in0=rsqrt_c[:], scalar1=D_MAX)
-        d_rep = keep.tile([P, PACK, P], F32)
+        d_col = keep.tile([P, PACK], F32)
         nc.vector.scalar_tensor_tensor(
-            out=d_rep[:],
-            in0=c_col.unsqueeze(2).to_broadcast([P, PACK, P]),
-            scalar=0.0,
-            in1=rsqrt_cap[:].unsqueeze(2).to_broadcast([P, PACK, P]),
-            op0=ALU.is_gt,
-            op1=ALU.mult,
+            out=d_col[:], in0=c_col, scalar=0.0, in1=rsqrt_cap[:], op0=ALU.is_gt, op1=ALU.mult
         )
-        d_row = ps_head.tile([P, PACK, P], F32)
+
+        d_rep = keep.tile([P, PACK, P], F32)
+        nc.scalar.activation(
+            out=d_rep[:], in_=d_col[:].unsqueeze(2).to_broadcast([P, PACK, P]), func=ACT.Copy
+        )
+        b2_ps = psum.tile([P, P], BF16, tag="rest")
+        nc.tensor.transpose(b2_ps[:], b2_rows[:], ident_b[:])
+        d_row = psum.tile([P, PACK, P], F32, tag="rest")
         for t in range(PACK):
             nc.tensor.transpose(d_row[:, t, :], d_rep[:, t, :], ident_f[:])
 
-        msg_grp = keep.tile([P, HIDDEN, PACK], BF16, align_bytes=64)
-        regroup(nc, msg_grp[:], msg_sb[:])
-        msg_codes, msg_scales = quantise(nc, keep, "msg", msg_grp[:])
+        msg_grp = regroup(nc, keep, "msg_grp", msg_sb[:])
+        msg_codes, msg_scales = quantise(nc, keep, "msg", msg_grp)
+        b2_col = keep.tile([P, PACK], F32)
+        nc.vector.tensor_copy(out=b2_col[:], in_=b2_ps[:, 0:PACK])
 
-        h_banks = []
-        for t in range(CHUNKS):
-            cols = slice(t * CHUNK, (t + 1) * CHUNK)
-            adj_dj = work.tile([P, PACK, CHUNK], F32)
+        def scale_by_dj(t):
+            adj_dj = work.tile([P, PACK, CHUNK], F32, name="adj_dj")
             for q in range(PACK):
                 nc.scalar.activation(
-                    out=adj_dj[:, q, :], in_=adj_sb[:, q, cols], func=ACT.Copy, scale=d_rep[:, q, 0:1]
+                    out=adj_dj[:, q, :],
+                    in_=adj_sb[:, q, t * CHUNK : (t + 1) * CHUNK],
+                    func=ACT.Copy,
+                    scale=d_col[:, q : q + 1],
                 )
-            a_grp = work.tile([P, CHUNK, PACK], BF16, align_bytes=64)
+            return adj_dj
+
+        def scale_by_di(t, adj_dj):
+            a_grp = work.tile([P, CHUNK, PACK], BF16, name="a_grp", align_bytes=64)
+            d_row_t = d_row[:].rearrange("p t n -> p (t n)")[:, t * CHUNK : (t + 1) * CHUNK]
             nc.vector.tensor_tensor(
                 out=a_grp[:],
                 in0=adj_dj[:].rearrange("p q c -> p c q"),
-                in1=d_row[:, t, :].unsqueeze(2).to_broadcast([P, CHUNK, PACK]),
+                in1=d_row_t.unsqueeze(2).to_broadcast([P, CHUNK, PACK]),
                 op=ALU.mult,
             )
-            a_codes, a_scales = quantise(nc, work, "a", a_grp[:])
-            h_ps = ps_h.tile([P, PACK, CHUNK], F32)
-            for q in range(PACK):
-                f_cols = slice(q * P, (q + 1) * P)
+            return a_grp
+
+        def hidden(a_grp):
+            a_codes, a_scales = quantise(nc, work, "a", a_grp)
+            h_planes = work.tile([P, PACK, CHUNK], BF16, name="h_planes")
+            for b in range(PACK // PLANES_PER_BANK):
+                h_ps = psum.tile([P, PLANES_PER_BANK, CHUNK], F32, name="h_ps")
+                for r in range(PLANES_PER_BANK):
+                    q = b * PLANES_PER_BANK + r
+                    nc.tensor.matmul_mx(
+                        out=h_ps[:, r, :],
+                        lhsT=msg_codes[:, q * P : (q + 1) * P].bitcast(FP8X4),
+                        lhsT_scale=msg_scales[:, q * P : (q + 1) * P],
+                        rhs=a_codes[:].bitcast(FP8X4),
+                        rhs_scale=a_scales[:],
+                        start=True,
+                        stop=True,
+                    )
+                for r in range(PLANES_PER_BANK):
+                    q = b * PLANES_PER_BANK + r
+                    nc.scalar.activation(
+                        out=h_planes[:, q, :], in_=h_ps[:, r, :], func=ACT.Relu, bias=b2_col[:, q : q + 1]
+                    )
+            return h_planes
+
+        adj_dj = [scale_by_dj(t) for t in range(CHUNKS)]
+        a_grp = [scale_by_di(0, adj_dj[0])]
+        h_planes = []
+        for t in range(CHUNKS):
+            if t + 1 < CHUNKS:
+                a_grp.append(scale_by_di(t + 1, adj_dj[t + 1]))
+            h_planes.append(hidden(a_grp[t]))
+
+        def project(h_grp_t):
+            h_codes, h_scales = quantise(nc, work, "h", h_grp_t)
+            banks = []
+            for s in range(CHUNK // P):
+                o_ps = psum.tile([P, DOUT], F32, name="o_ps", tag="rest")
                 nc.tensor.matmul_mx(
-                    out=h_ps[:, q, :],
-                    lhsT=msg_codes[:, f_cols].bitcast(FP8X4),
-                    lhsT_scale=msg_scales[:, f_cols],
-                    rhs=a_codes[:].bitcast(FP8X4),
-                    rhs_scale=a_scales[:],
+                    out=o_ps[:],
+                    lhsT=h_codes[:, s * P : (s + 1) * P].bitcast(FP8X4),
+                    lhsT_scale=h_scales[:, s * P : (s + 1) * P],
+                    rhs=w3_codes[:].bitcast(FP8X4),
+                    rhs_scale=w3_scales[:],
                     start=True,
                     stop=True,
                 )
-            h_banks.append(h_ps)
-            if t == 1:
-                w3_grp = keep.tile([P, DOUT, PACK], BF16, align_bytes=64)
-                regroup(nc, w3_grp[:], w3_sb[:])
-                w3_codes, w3_scales = quantise(nc, keep, "w3", w3_grp[:])
+                banks.append(o_ps)
+            return banks
 
+        def store(t, banks):
+            for s in range(CHUNK // P):
+                first = t * CHUNK + s * P
+                o_sb = work.tile([P, DOUT], F32, name="o_sb", bufs=NODES // P)
+                if first + P < NODES:
+                    nc.scalar.copy(out=o_sb[:], in_=banks[s][:])
+                else:
+                    nc.vector.tensor_copy(out=o_sb[:], in_=banks[s][:])
+                nc.sync.dma_start(out=out[0, first : first + P, :], in_=o_sb[:])
+
+        w3_grp = regroup(nc, keep, "w3_grp", w3_sb[:])
+        h_grp = [regroup(nc, work, "h_grp", h_planes[0][:])]
+        w3_codes, w3_scales = quantise(nc, keep, "w3", w3_grp)
+        o_banks = []
         for t in range(CHUNKS):
-            h_ps = h_banks[t]
-            h_planes = work.tile([P, PACK, CHUNK], BF16)
-            for q in range(PACK):
-                nc.scalar.activation(
-                    out=h_planes[:, q, :], in_=h_ps[:, q, :], func=ACT.Relu, bias=b2_col[:, q : q + 1]
-                )
-            h_grp = work.tile([P, CHUNK, PACK], BF16, align_bytes=64)
-            regroup(nc, h_grp[:], h_planes[:])
-            h_codes, h_scales = quantise(nc, work, "h", h_grp[:])
-            o_ps = ps_o.tile([P, DOUT], F32)
-            nc.tensor.matmul_mx(
-                out=o_ps[:],
-                lhsT=h_codes[:].bitcast(FP8X4),
-                lhsT_scale=h_scales[:],
-                rhs=w3_codes[:].bitcast(FP8X4),
-                rhs_scale=w3_scales[:],
-                start=True,
-                stop=True,
-            )
-            o_sb = work.tile([P, DOUT], F32)
-            nc.scalar.copy(out=o_sb[:], in_=o_ps[:])
-            nc.sync.dma_start(out=out[0, t * CHUNK : (t + 1) * CHUNK, :], in_=o_sb[:])
+            if t + 1 < CHUNKS:
+                h_grp.append(regroup(nc, work, "h_grp", h_planes[t + 1][:]))
+            o_banks.append(project(h_grp[t]))
+            if t >= 1:
+                store(t - 1, o_banks[t - 1])
+        store(CHUNKS - 1, o_banks[CHUNKS - 1])

@@ -31,13 +31,11 @@ def load_k_first(nc, pool, name, rows):
     return planes
 
 
-def regroup(nc, pool, name, planes):
-    grouped = pool.tile([P, planes.shape[2], PACK], BF16, name=name, align_bytes=64)
-    nc.vector.tensor_copy(
-        out=grouped[:].rearrange("p (c i) q -> p c q i", i=4),
+def regroup(copy, grouped, planes):
+    copy(
+        out=grouped.rearrange("p (c i) q -> p c q i", i=4),
         in_=planes.rearrange("p q (c i) -> p c q i", i=4),
     )
-    return grouped
 
 
 def quantise(nc, pool, name, grouped):
@@ -60,7 +58,11 @@ def tile_perception_pb_s_kernel(tc, msg, adj, b2, W3, out):
         work = ctx.enter_context(tc.tile_pool(name="work", bufs=CHUNKS))
         psum = ctx.enter_context(tc.psum_pool(name="psum", bufs=4))
 
-        adj_sb = load_k_first(nc, keep, "adj_sb", adj[0])
+        adj_sb = []
+        for q in range(PACK):
+            adj_plane = keep.tile([P, NODES], BF16, name="adj_plane%d" % q)
+            nc.sync.dma_start(out=adj_plane[:], in_=adj[0, q * P : (q + 1) * P, :])
+            adj_sb.append(adj_plane)
         msg_sb = load_k_first(nc, keep, "msg_sb", msg[0])
         w3_sb = load_k_first(nc, keep, "w3_sb", W3)
         b2_rows = keep.tile([P, P], BF16)
@@ -78,25 +80,28 @@ def tile_perception_pb_s_kernel(tc, msg, adj, b2, W3, out):
         table_warm = keep.tile([P, 1], F32)
         nc.scalar.activation(out=table_warm[:], in_=one_col[:], func=ACT.Abs_reciprocal_sqrt)
 
-        c_ps = psum.tile([P, PACK, ONES_COLS], F32, tag="rest")
-        for t in range(PACK):
-            for q in range(PACK):
+        c_ps = psum.tile([P, PACK, PACK, ONES_COLS], F32, tag="rest")
+        for q in range(PACK):
+            for t in range(PACK):
                 nc.tensor.matmul(
-                    out=c_ps[:, t, :],
-                    lhsT=adj_sb[:, q, t * P : (t + 1) * P],
+                    out=c_ps[:, q, t, :],
+                    lhsT=adj_sb[q][:, t * P : (t + 1) * P],
                     rhs=ones[:],
-                    start=(q == 0),
-                    stop=(q == PACK - 1),
+                    start=True,
+                    stop=True,
                 )
-        c_col = c_ps[:, :, 0]
+        c_col = keep.tile([P, PACK], F32)
+        nc.vector.tensor_reduce(
+            out=c_col[:], in_=c_ps[:, :, :, 0].rearrange("p q t -> p t q"), axis=mybir.AxisListType.X, op=ALU.add
+        )
 
         rsqrt_c = keep.tile([P, PACK], F32)
-        nc.scalar.activation(out=rsqrt_c[:], in_=c_col, func=ACT.Abs_reciprocal_sqrt)
-        rsqrt_cap = keep.tile([P, PACK], F32)
-        nc.vector.tensor_scalar_min(out=rsqrt_cap[:], in0=rsqrt_c[:], scalar1=D_MAX)
+        nc.scalar.activation(out=rsqrt_c[:], in_=c_col[:], func=ACT.Abs_reciprocal_sqrt)
+        c_positive = keep.tile([P, PACK], F32)
+        nc.vector.tensor_single_scalar(out=c_positive[:], in_=c_col[:], scalar=0.0, op=ALU.is_gt)
         d_col = keep.tile([P, PACK], F32)
         nc.vector.scalar_tensor_tensor(
-            out=d_col[:], in0=c_col, scalar=0.0, in1=rsqrt_cap[:], op0=ALU.is_gt, op1=ALU.mult
+            out=d_col[:], in0=rsqrt_c[:], scalar=D_MAX, in1=c_positive[:], op0=ALU.min, op1=ALU.mult
         )
 
         d_rep = keep.tile([P, PACK, P], F32)
@@ -109,7 +114,8 @@ def tile_perception_pb_s_kernel(tc, msg, adj, b2, W3, out):
         for t in range(PACK):
             nc.tensor.transpose(d_row[:, t, :], d_rep[:, t, :], ident_f[:])
 
-        msg_grp = regroup(nc, keep, "msg_grp", msg_sb[:])
+        msg_grp = keep.tile([P, HIDDEN, PACK], BF16, align_bytes=64)
+        regroup(nc.vector.tensor_copy, msg_grp[:], msg_sb[:])
         msg_codes, msg_scales = quantise(nc, keep, "msg", msg_grp)
         b2_col = keep.tile([P, PACK], F32)
         nc.vector.tensor_copy(out=b2_col[:], in_=b2_ps[:, 0:PACK])
@@ -119,7 +125,7 @@ def tile_perception_pb_s_kernel(tc, msg, adj, b2, W3, out):
             for q in range(PACK):
                 nc.scalar.activation(
                     out=adj_dj[:, q, :],
-                    in_=adj_sb[:, q, t * CHUNK : (t + 1) * CHUNK],
+                    in_=adj_sb[q][:, t * CHUNK : (t + 1) * CHUNK],
                     func=ACT.Copy,
                     scale=d_col[:, q : q + 1],
                 )
@@ -160,6 +166,8 @@ def tile_perception_pb_s_kernel(tc, msg, adj, b2, W3, out):
             return h_planes
 
         adj_dj = [scale_by_dj(t) for t in range(CHUNKS)]
+        w3_grp = keep.tile([P, DOUT, PACK], BF16, align_bytes=64)
+        regroup(nc.scalar.copy, w3_grp[:, 0 : DOUT // 2, :], w3_sb[:, :, 0 : DOUT // 2])
         a_grp = [scale_by_di(0, adj_dj[0])]
         h_planes = []
         for t in range(CHUNKS):
@@ -194,13 +202,18 @@ def tile_perception_pb_s_kernel(tc, msg, adj, b2, W3, out):
                     nc.vector.tensor_copy(out=o_sb[:], in_=banks[s][:])
                 nc.sync.dma_start(out=out[0, first : first + P, :], in_=o_sb[:])
 
-        w3_grp = regroup(nc, keep, "w3_grp", w3_sb[:])
-        h_grp = [regroup(nc, work, "h_grp", h_planes[0][:])]
+        def regroup_hidden(t):
+            h_grp_t = work.tile([P, CHUNK, PACK], BF16, name="h_grp", align_bytes=64)
+            regroup(nc.vector.tensor_copy, h_grp_t[:], h_planes[t][:])
+            return h_grp_t
+
+        regroup(nc.vector.tensor_copy, w3_grp[:, DOUT // 2 : DOUT, :], w3_sb[:, :, DOUT // 2 : DOUT])
+        h_grp = [regroup_hidden(0)]
         w3_codes, w3_scales = quantise(nc, keep, "w3", w3_grp)
         o_banks = []
         for t in range(CHUNKS):
             if t + 1 < CHUNKS:
-                h_grp.append(regroup(nc, work, "h_grp", h_planes[t + 1][:]))
+                h_grp.append(regroup_hidden(t + 1))
             o_banks.append(project(h_grp[t]))
             if t >= 1:
                 store(t - 1, o_banks[t - 1])

@@ -20,6 +20,8 @@ CHUNK = 128
 CHUNKS = NODES // CHUNK
 PLANES_PER_BANK = 512 // CHUNK
 ONES_COLS = 32
+HALF = DOUT // 2
+VECTOR_BANKS = 3
 D_MAX = 1e15
 
 FLOPS = 2 * NODES * NODES * HIDDEN + 2 * NODES * HIDDEN * DOUT
@@ -56,7 +58,7 @@ def tile_perception_pb_s_kernel(tc, msg, adj, b2, W3, out):
         ctx.enter_context(tc.manual_schedule())
         keep = ctx.enter_context(tc.tile_pool(name="keep", bufs=1))
         work = ctx.enter_context(tc.tile_pool(name="work", bufs=CHUNKS))
-        psum = ctx.enter_context(tc.psum_pool(name="psum", bufs=4))
+        psum = ctx.enter_context(tc.psum_pool(name="psum", bufs=8))
 
         adj_sb = []
         for q in range(PACK):
@@ -80,7 +82,7 @@ def tile_perception_pb_s_kernel(tc, msg, adj, b2, W3, out):
         table_warm = keep.tile([P, 1], F32)
         nc.scalar.activation(out=table_warm[:], in_=one_col[:], func=ACT.Abs_reciprocal_sqrt)
 
-        c_ps = psum.tile([P, PACK, PACK, ONES_COLS], F32, tag="rest")
+        c_ps = psum.tile([P, PACK, PACK, ONES_COLS], F32, tag="bank")
         for q in range(PACK):
             for t in range(PACK):
                 nc.tensor.matmul(
@@ -108,9 +110,9 @@ def tile_perception_pb_s_kernel(tc, msg, adj, b2, W3, out):
         nc.scalar.activation(
             out=d_rep[:], in_=d_col[:].unsqueeze(2).to_broadcast([P, PACK, P]), func=ACT.Copy
         )
-        b2_ps = psum.tile([P, P], BF16, tag="rest")
+        b2_ps = psum.tile([P, P], BF16, tag="bank")
         nc.tensor.transpose(b2_ps[:], b2_rows[:], ident_b[:])
-        d_row = psum.tile([P, PACK, P], F32, tag="rest")
+        d_row = psum.tile([P, PACK, P], F32, tag="bank")
         for t in range(PACK):
             nc.tensor.transpose(d_row[:, t, :], d_rep[:, t, :], ident_f[:])
 
@@ -146,7 +148,7 @@ def tile_perception_pb_s_kernel(tc, msg, adj, b2, W3, out):
             a_codes, a_scales = quantise(nc, work, "a", a_grp)
             h_planes = work.tile([P, PACK, CHUNK], BF16, name="h_planes")
             for b in range(PACK // PLANES_PER_BANK):
-                h_ps = psum.tile([P, PLANES_PER_BANK, CHUNK], F32, name="h_ps")
+                h_ps = psum.tile([P, PLANES_PER_BANK, CHUNK], F32, name="h_ps", tag="bank")
                 for r in range(PLANES_PER_BANK):
                     q = b * PLANES_PER_BANK + r
                     nc.tensor.matmul_mx(
@@ -178,14 +180,15 @@ def tile_perception_pb_s_kernel(tc, msg, adj, b2, W3, out):
         def project(h_grp_t):
             h_codes, h_scales = quantise(nc, work, "h", h_grp_t)
             banks = []
-            for s in range(CHUNK // P):
-                o_ps = psum.tile([P, DOUT], F32, name="o_ps", tag="rest")
+            for half in range(2):
+                o_cols = slice(half * HALF, (half + 1) * HALF)
+                o_ps = psum.tile([P, HALF], F32, name="o_ps", tag="bank")
                 nc.tensor.matmul_mx(
                     out=o_ps[:],
-                    lhsT=h_codes[:, s * P : (s + 1) * P].bitcast(FP8X4),
-                    lhsT_scale=h_scales[:, s * P : (s + 1) * P],
-                    rhs=w3_codes[:].bitcast(FP8X4),
-                    rhs_scale=w3_scales[:],
+                    lhsT=h_codes[:].bitcast(FP8X4),
+                    lhsT_scale=h_scales[:],
+                    rhs=w3_codes[:, o_cols].bitcast(FP8X4),
+                    rhs_scale=w3_scales[:, o_cols],
                     start=True,
                     stop=True,
                 )
@@ -193,14 +196,15 @@ def tile_perception_pb_s_kernel(tc, msg, adj, b2, W3, out):
             return banks
 
         def store(t, banks):
-            for s in range(CHUNK // P):
-                first = t * CHUNK + s * P
-                o_sb = work.tile([P, DOUT], F32, name="o_sb", bufs=NODES // P)
-                if first + P < NODES:
-                    nc.scalar.copy(out=o_sb[:], in_=banks[s][:])
+            for half in range(2):
+                o_sb = work.tile([P, HALF], F32, name="o_sb", bufs=2 * CHUNKS)
+                if 2 * t + half < 2 * CHUNKS - VECTOR_BANKS:
+                    nc.scalar.copy(out=o_sb[:], in_=banks[half][:])
                 else:
-                    nc.vector.tensor_copy(out=o_sb[:], in_=banks[s][:])
-                nc.sync.dma_start(out=out[0, first : first + P, :], in_=o_sb[:])
+                    nc.vector.tensor_copy(out=o_sb[:], in_=banks[half][:])
+                nc.sync.dma_start(
+                    out=out[0, t * CHUNK : (t + 1) * CHUNK, half * HALF : (half + 1) * HALF], in_=o_sb[:]
+                )
 
         def regroup_hidden(t):
             h_grp_t = work.tile([P, CHUNK, PACK], BF16, name="h_grp", align_bytes=64)

@@ -106,15 +106,12 @@ def tile_perception_pb_s_kernel(tc, msg, adj, b2, W3, out):
             out=d_col[:], in0=rsqrt_c[:], scalar=D_MAX, in1=c_positive[:], op0=ALU.min, op1=ALU.mult
         )
 
-        d_rep = keep.tile([P, PACK, P], F32)
-        nc.scalar.activation(
-            out=d_rep[:], in_=d_col[:].unsqueeze(2).to_broadcast([P, PACK, P]), func=ACT.Copy
-        )
         b2_ps = psum.tile([P, P], BF16, tag="bank")
         nc.tensor.transpose(b2_ps[:], b2_rows[:], ident_b[:])
+
         d_row = psum.tile([P, PACK, P], F32, tag="bank")
         for t in range(PACK):
-            nc.tensor.transpose(d_row[:, t, :], d_rep[:, t, :], ident_f[:])
+            nc.tensor.transpose(d_row[:, t, :], d_col[:, t : t + 1].to_broadcast([P, P]), ident_f[:])
 
         msg_grp = keep.tile([P, HIDDEN, PACK], BF16, align_bytes=64)
         regroup(nc.vector.tensor_copy, msg_grp[:], msg_sb[:])

@@ -19,18 +19,12 @@ DOUT = 512
 CHUNK = 128
 CHUNKS = NODES // CHUNK
 PLANES_PER_BANK = 512 // CHUNK
-ONES_COLS = 32
+WARM_PASSES = 4
+COUNT_COLS = 2
 HALF = DOUT // 2
 VECTOR_BANKS = 3
-D_MAX = 1e15
 
 FLOPS = 2 * NODES * NODES * HIDDEN + 2 * NODES * HIDDEN * DOUT
-
-
-def load_k_first(nc, pool, name, rows):
-    planes = pool.tile([P, PACK, rows.shape[1]], BF16, name=name)
-    nc.sync.dma_start(out=planes[:], in_=rows.rearrange("(q p) w -> p q w", p=P))
-    return planes
 
 
 def regroup(copy, grouped, planes):
@@ -60,83 +54,96 @@ def tile_perception_pb_s_kernel(tc, msg, adj, b2, W3, out):
         work = ctx.enter_context(tc.tile_pool(name="work", bufs=CHUNKS))
         psum = ctx.enter_context(tc.psum_pool(name="psum", bufs=8))
 
-        adj_sb = []
-        for q in range(PACK):
-            adj_plane = keep.tile([P, NODES], BF16, name="adj_plane%d" % q)
-            nc.sync.dma_start(out=adj_plane[:], in_=adj[0, q * P : (q + 1) * P, :])
-            adj_sb.append(adj_plane)
-        msg_sb = load_k_first(nc, keep, "msg_sb", msg[0])
-        w3_sb = load_k_first(nc, keep, "w3_sb", W3)
+        adj_sb = keep.tile([P, PACK, NODES], BF16)
+        adj_slots = adj[0].rearrange("(p t) i -> t p i", t=PACK)
+        for t in range(PACK):
+            nc.sync.dma_start(out=adj_sb[:, t, :], in_=adj_slots[t])
+        msg_sb = keep.tile([P, PACK, HIDDEN], BF16)
+        nc.sync.dma_start(out=msg_sb[:], in_=msg[0].rearrange("(p t) f -> p t f", t=PACK))
+        w3_sb = keep.tile([P, PACK, DOUT], BF16)
+        nc.sync.dma_start(out=w3_sb[:], in_=W3.rearrange("(q p) o -> p q o", p=P))
         b2_rows = keep.tile([P, P], BF16)
         nc.vector.memset(b2_rows[:], 0.0)
+        warm_in = keep.tile([P, P], F32)
+        nc.vector.memset(warm_in[:], 1.0)
         nc.scalar.dma_start(out=b2_rows[0:PACK, :], in_=b2.rearrange("(q p) -> q p", p=P))
 
+        ones = keep.tile([P, P], BF16)
+        nc.vector.memset(ones[:], 1.0)
+        one_col = keep.tile([P, 1], F32)
+        nc.vector.memset(one_col[:], 1.0)
         ident_f = keep.tile([P, P], F32)
         make_identity(nc, ident_f[:])
         ident_b = keep.tile([P, P], BF16)
         make_identity(nc, ident_b[:])
-        ones = keep.tile([P, ONES_COLS], BF16)
-        nc.vector.memset(ones[:], 1.0)
-        one_col = keep.tile([P, 1], F32)
-        nc.vector.memset(one_col[:], 1.0)
         table_warm = keep.tile([P, 1], F32)
         nc.scalar.activation(out=table_warm[:], in_=one_col[:], func=ACT.Abs_reciprocal_sqrt)
 
-        c_ps = psum.tile([P, PACK, PACK, ONES_COLS], F32, tag="bank")
-        for q in range(PACK):
-            for t in range(PACK):
+        warm_ps = psum.tile([P, P], F32, tag="bank")
+        for repeat in range(WARM_PASSES):
+            nc.tensor.matmul(out=warm_ps[:], lhsT=warm_in[:], rhs=warm_in[:], start=True, stop=True)
+
+        col_ps = psum.tile([P, 2, CHUNKS, COUNT_COLS], F32, tag="bank")
+        row_ps = psum.tile([P, NODES], F32, tag="bank")
+        pair_sums = []
+        for pair in range(2):
+            pair_sum = keep.tile([P, NODES], BF16, name="pair_sum%d" % pair)
+            nc.vector.tensor_tensor(
+                out=pair_sum[:], in0=adj_sb[:, 2 * pair, :], in1=adj_sb[:, 2 * pair + 1, :], op=ALU.add
+            )
+            pair_sums.append(pair_sum)
+
+        def row_sums(pair):
+            nc.tensor.matmul(out=row_ps[:], lhsT=ones[:], rhs=pair_sums[pair][:], start=(pair == 0), stop=(pair == 1))
+
+        def column_sums(pair):
+            for k in range(CHUNKS):
                 nc.tensor.matmul(
-                    out=c_ps[:, q, t, :],
-                    lhsT=adj_sb[q][:, t * P : (t + 1) * P],
-                    rhs=ones[:],
+                    out=col_ps[:, pair, k, :],
+                    lhsT=pair_sums[pair][:, k * CHUNK : (k + 1) * CHUNK],
+                    rhs=ones[:, 0:COUNT_COLS],
                     start=True,
                     stop=True,
                 )
-        c_col = keep.tile([P, PACK], F32)
+
+        row_sums(0)
+        column_sums(0)
+        column_sums(1)
+        row_sums(1)
+
+        adj_grp = keep.tile([P, NODES, PACK], BF16, align_bytes=64)
+
+        def regroup_adj(copy, k):
+            cols = slice(k * CHUNK, (k + 1) * CHUNK)
+            regroup(copy, adj_grp[:, cols, :], adj_sb[:, :, cols])
+
+        for k in range(2, CHUNKS):
+            regroup_adj(nc.scalar.copy, k)
+        for k in range(2):
+            regroup_adj(nc.vector.tensor_copy, k)
+        c_col = keep.tile([P, CHUNKS], F32)
         nc.vector.tensor_reduce(
-            out=c_col[:], in_=c_ps[:, :, :, 0].rearrange("p q t -> p t q"), axis=mybir.AxisListType.X, op=ALU.add
+            out=c_col[:], in_=col_ps[:, :, :, 0].rearrange("p s k -> p k s"), axis=mybir.AxisListType.X, op=ALU.add
         )
-
-        rsqrt_c = keep.tile([P, PACK], F32)
-        nc.scalar.activation(out=rsqrt_c[:], in_=c_col[:], func=ACT.Abs_reciprocal_sqrt)
-        c_positive = keep.tile([P, PACK], F32)
-        nc.vector.tensor_single_scalar(out=c_positive[:], in_=c_col[:], scalar=0.0, op=ALU.is_gt)
-        d_col = keep.tile([P, PACK], F32)
-        nc.vector.scalar_tensor_tensor(
-            out=d_col[:], in0=rsqrt_c[:], scalar=D_MAX, in1=c_positive[:], op0=ALU.min, op1=ALU.mult
-        )
-
-        b2_ps = psum.tile([P, P], BF16, tag="bank")
-        nc.tensor.transpose(b2_ps[:], b2_rows[:], ident_b[:])
-
-        d_row = psum.tile([P, PACK, P], F32, tag="bank")
-        for t in range(PACK):
-            nc.tensor.transpose(d_row[:, t, :], d_col[:, t : t + 1].to_broadcast([P, P]), ident_f[:])
 
         msg_grp = keep.tile([P, HIDDEN, PACK], BF16, align_bytes=64)
         regroup(nc.vector.tensor_copy, msg_grp[:], msg_sb[:])
-        msg_codes, msg_scales = quantise(nc, keep, "msg", msg_grp)
-        b2_col = keep.tile([P, PACK], F32)
-        nc.vector.tensor_copy(out=b2_col[:], in_=b2_ps[:, 0:PACK])
 
-        def scale_by_dj(t):
-            adj_dj = work.tile([P, PACK, CHUNK], F32, name="adj_dj")
-            for q in range(PACK):
-                nc.scalar.activation(
-                    out=adj_dj[:, q, :],
-                    in_=adj_sb[q][:, t * CHUNK : (t + 1) * CHUNK],
-                    func=ACT.Copy,
-                    scale=d_col[:, q : q + 1],
-                )
-            return adj_dj
+        def outer_product(k):
+            dd = work.tile([P, NODES], BF16, name="dd")
+            nc.scalar.activation(out=dd[:], in_=row_ps[:], func=ACT.Abs_reciprocal_sqrt, scale=c_col[:, k : k + 1])
+            dd_ps = psum.tile([P, 2, CHUNK], F32, name="dd_ps", tag="bank")
+            words = dd[:].bitcast(F32)
+            for u in range(2):
+                nc.tensor.transpose(dd_ps[:, u, :], words[:, u : NODES // 2 : 2], ident_f[:])
+            return dd_ps
 
-        def scale_by_di(t, adj_dj):
+        def scaled(k, dd_ps):
             a_grp = work.tile([P, CHUNK, PACK], BF16, name="a_grp", align_bytes=64)
-            d_row_t = d_row[:].rearrange("p t n -> p (t n)")[:, t * CHUNK : (t + 1) * CHUNK]
             nc.vector.tensor_tensor(
-                out=a_grp[:],
-                in0=adj_dj[:].rearrange("p q c -> p c q"),
-                in1=d_row_t.unsqueeze(2).to_broadcast([P, CHUNK, PACK]),
+                out=a_grp[:].rearrange("p n (u e) -> p n u e", e=2),
+                in0=adj_grp[:, k * CHUNK : (k + 1) * CHUNK, :].rearrange("p n (u e) -> p n u e", e=2),
+                in1=dd_ps[:].bitcast(BF16).rearrange("p u (n e) -> p n u e", e=2),
                 op=ALU.mult,
             )
             return a_grp
@@ -164,14 +171,21 @@ def tile_perception_pb_s_kernel(tc, msg, adj, b2, W3, out):
                     )
             return h_planes
 
-        adj_dj = [scale_by_dj(t) for t in range(CHUNKS)]
+        dd_banks = [outer_product(0)]
+        b2_ps = psum.tile([P, P], BF16, tag="bank")
+        nc.tensor.transpose(b2_ps[:], b2_rows[:], ident_b[:])
+        dd_banks += [outer_product(k) for k in range(1, CHUNKS)]
         w3_grp = keep.tile([P, DOUT, PACK], BF16, align_bytes=64)
         regroup(nc.scalar.copy, w3_grp[:, 0 : DOUT // 2, :], w3_sb[:, :, 0 : DOUT // 2])
-        a_grp = [scale_by_di(0, adj_dj[0])]
+        msg_codes, msg_scales = quantise(nc, keep, "msg", msg_grp)
+        a_grp = [scaled(0, dd_banks[0])]
+        b2_col = keep.tile([P, PACK], F32)
         h_planes = []
         for t in range(CHUNKS):
             if t + 1 < CHUNKS:
-                a_grp.append(scale_by_di(t + 1, adj_dj[t + 1]))
+                a_grp.append(scaled(t + 1, dd_banks[t + 1]))
+            if t == 0:
+                nc.vector.tensor_copy(out=b2_col[:], in_=b2_ps[:, 0:PACK])
             h_planes.append(hidden(a_grp[t]))
 
         def project(h_grp_t):

@@ -19,7 +19,7 @@ DOUT = 512
 CHUNK = 128
 CHUNKS = NODES // CHUNK
 PLANES_PER_BANK = 512 // CHUNK
-WARM_PASSES = 4
+WARM_PASSES = 3
 COUNT_COLS = 2
 HALF = DOUT // 2
 VECTOR_BANKS = 3
@@ -55,11 +55,17 @@ def tile_perception_pb_s_kernel(tc, msg, adj, b2, W3, out):
         psum = ctx.enter_context(tc.psum_pool(name="psum", bufs=8))
 
         adj_sb = keep.tile([P, PACK, NODES], BF16)
-        adj_slots = adj[0].rearrange("(p t) i -> t p i", t=PACK)
-        for t in range(PACK):
-            nc.sync.dma_start(out=adj_sb[:, t, :], in_=adj_slots[t])
+        for u in range(2):
+            nc.sync.dma_start(
+                out=adj_sb[:, 2 * u : 2 * u + 2, :],
+                in_=adj[0, u * 2 * P : (u + 1) * 2 * P, :].rearrange("(p e) i -> p e i", e=2),
+            )
         msg_sb = keep.tile([P, PACK, HIDDEN], BF16)
-        nc.sync.dma_start(out=msg_sb[:], in_=msg[0].rearrange("(p t) f -> p t f", t=PACK))
+        for u in range(2):
+            nc.sync.dma_start(
+                out=msg_sb[:, 2 * u : 2 * u + 2, :],
+                in_=msg[0, u * 2 * P : (u + 1) * 2 * P, :].rearrange("(p e) f -> p e f", e=2),
+            )
         w3_sb = keep.tile([P, PACK, DOUT], BF16)
         nc.sync.dma_start(out=w3_sb[:], in_=W3.rearrange("(q p) o -> p q o", p=P))
         b2_rows = keep.tile([P, P], BF16)
@@ -117,14 +123,14 @@ def tile_perception_pb_s_kernel(tc, msg, adj, b2, W3, out):
             cols = slice(k * CHUNK, (k + 1) * CHUNK)
             regroup(copy, adj_grp[:, cols, :], adj_sb[:, :, cols])
 
-        for k in range(2, CHUNKS):
-            regroup_adj(nc.scalar.copy, k)
+        regroup_adj(nc.scalar.copy, CHUNKS - 1)
         for k in range(2):
             regroup_adj(nc.vector.tensor_copy, k)
         c_col = keep.tile([P, CHUNKS], F32)
         nc.vector.tensor_reduce(
             out=c_col[:], in_=col_ps[:, :, :, 0].rearrange("p s k -> p k s"), axis=mybir.AxisListType.X, op=ALU.add
         )
+        regroup_adj(nc.vector.tensor_copy, 2)
 
         msg_grp = keep.tile([P, HIDDEN, PACK], BF16, align_bytes=64)
         regroup(nc.vector.tensor_copy, msg_grp[:], msg_sb[:])
@@ -135,7 +141,7 @@ def tile_perception_pb_s_kernel(tc, msg, adj, b2, W3, out):
             dd_ps = psum.tile([P, 2, CHUNK], F32, name="dd_ps", tag="bank")
             words = dd[:].bitcast(F32)
             for u in range(2):
-                nc.tensor.transpose(dd_ps[:, u, :], words[:, u : NODES // 2 : 2], ident_f[:])
+                nc.tensor.transpose(dd_ps[:, u, :], words[:, u * P : (u + 1) * P], ident_f[:])
             return dd_ps
 
         def scaled(k, dd_ps):

@@ -70,8 +70,6 @@ def tile_perception_pb_s_kernel(tc, msg, adj, b2, W3, out):
         nc.sync.dma_start(out=w3_sb[:], in_=W3.rearrange("(q p) o -> p q o", p=P))
         b2_rows = keep.tile([P, P], BF16)
         nc.vector.memset(b2_rows[:], 0.0)
-        warm_in = keep.tile([P, P], F32)
-        nc.vector.memset(warm_in[:], 1.0)
         nc.scalar.dma_start(out=b2_rows[0:PACK, :], in_=b2.rearrange("(q p) -> q p", p=P))
 
         ones = keep.tile([P, P], BF16)
@@ -87,7 +85,7 @@ def tile_perception_pb_s_kernel(tc, msg, adj, b2, W3, out):
 
         warm_ps = psum.tile([P, P], F32, tag="bank")
         for repeat in range(WARM_PASSES):
-            nc.tensor.matmul(out=warm_ps[:], lhsT=warm_in[:], rhs=warm_in[:], start=True, stop=True)
+            nc.tensor.matmul(out=warm_ps[:], lhsT=ident_f[:], rhs=ident_f[:], start=True, stop=True)
 
         col_ps = psum.tile([P, 2, CHUNKS, COUNT_COLS], F32, tag="bank")
         row_ps = psum.tile([P, NODES], F32, tag="bank")
@@ -123,17 +121,20 @@ def tile_perception_pb_s_kernel(tc, msg, adj, b2, W3, out):
             cols = slice(k * CHUNK, (k + 1) * CHUNK)
             regroup(copy, adj_grp[:, cols, :], adj_sb[:, :, cols])
 
-        regroup_adj(nc.scalar.copy, CHUNKS - 1)
+        for k in range(2, CHUNKS):
+            regroup_adj(nc.scalar.copy, k)
         for k in range(2):
             regroup_adj(nc.vector.tensor_copy, k)
         c_col = keep.tile([P, CHUNKS], F32)
         nc.vector.tensor_reduce(
             out=c_col[:], in_=col_ps[:, :, :, 0].rearrange("p s k -> p k s"), axis=mybir.AxisListType.X, op=ALU.add
         )
-        regroup_adj(nc.vector.tensor_copy, 2)
 
-        msg_grp = keep.tile([P, HIDDEN, PACK], BF16, align_bytes=64)
-        regroup(nc.vector.tensor_copy, msg_grp[:], msg_sb[:])
+        msg_halves = [slice(0, HIDDEN // 2), slice(HIDDEN // 2, HIDDEN)]
+        msg_grp = [keep.tile([P, HIDDEN // 2, PACK], BF16, name="msg_grp%d" % m, align_bytes=64) for m in range(2)]
+        for m in range(2):
+            regroup(nc.vector.tensor_copy, msg_grp[m][:], msg_sb[:, :, msg_halves[m]])
+        msg_words = [quantise(nc, keep, "msg%d" % m, msg_grp[m]) for m in range(2)]
 
         def outer_product(k):
             dd = work.tile([P, NODES], BF16, name="dd")
@@ -161,10 +162,12 @@ def tile_perception_pb_s_kernel(tc, msg, adj, b2, W3, out):
                 h_ps = psum.tile([P, PLANES_PER_BANK, CHUNK], F32, name="h_ps", tag="bank")
                 for r in range(PLANES_PER_BANK):
                     q = b * PLANES_PER_BANK + r
+                    msg_codes, msg_scales = msg_words[q // 2]
+                    features = slice(q % 2 * P, (q % 2 + 1) * P)
                     nc.tensor.matmul_mx(
                         out=h_ps[:, r, :],
-                        lhsT=msg_codes[:, q * P : (q + 1) * P].bitcast(FP8X4),
-                        lhsT_scale=msg_scales[:, q * P : (q + 1) * P],
+                        lhsT=msg_codes[:, features].bitcast(FP8X4),
+                        lhsT_scale=msg_scales[:, features],
                         rhs=a_codes[:].bitcast(FP8X4),
                         rhs_scale=a_scales[:],
                         start=True,
@@ -183,7 +186,6 @@ def tile_perception_pb_s_kernel(tc, msg, adj, b2, W3, out):
         dd_banks += [outer_product(k) for k in range(1, CHUNKS)]
         w3_grp = keep.tile([P, DOUT, PACK], BF16, align_bytes=64)
         regroup(nc.scalar.copy, w3_grp[:, 0 : DOUT // 2, :], w3_sb[:, :, 0 : DOUT // 2])
-        msg_codes, msg_scales = quantise(nc, keep, "msg", msg_grp)
         a_grp = [scaled(0, dd_banks[0])]
         b2_col = keep.tile([P, PACK], F32)
         h_planes = []

@@ -22,7 +22,7 @@ PLANES_PER_BANK = 512 // CHUNK
 WARM_PASSES = 3
 COUNT_COLS = 2
 HALF = DOUT // 2
-VECTOR_BANKS = 3
+VECTOR_BANKS = ((2, 0), (2, 1), (3, 1))
 
 FLOPS = 2 * NODES * NODES * HIDDEN + 2 * NODES * HIDDEN * DOUT
 
@@ -217,10 +217,10 @@ def tile_perception_pb_s_kernel(tc, msg, adj, b2, W3, out):
         def store(t, banks):
             for half in range(2):
                 o_sb = work.tile([P, HALF], F32, name="o_sb", bufs=2 * CHUNKS)
-                if 2 * t + half < 2 * CHUNKS - VECTOR_BANKS:
-                    nc.scalar.copy(out=o_sb[:], in_=banks[half][:])
-                else:
+                if (t, half) in VECTOR_BANKS:
                     nc.vector.tensor_copy(out=o_sb[:], in_=banks[half][:])
+                else:
+                    nc.scalar.copy(out=o_sb[:], in_=banks[half][:])
                 nc.sync.dma_start(
                     out=out[0, t * CHUNK : (t + 1) * CHUNK, half * HALF : (half + 1) * HALF], in_=o_sb[:]
                 )
@@ -233,11 +233,11 @@ def tile_perception_pb_s_kernel(tc, msg, adj, b2, W3, out):
         regroup(nc.vector.tensor_copy, w3_grp[:, DOUT // 2 : DOUT, :], w3_sb[:, :, DOUT // 2 : DOUT])
         h_grp = [regroup_hidden(0)]
         w3_codes, w3_scales = quantise(nc, keep, "w3", w3_grp)
-        o_banks = []
-        for t in range(CHUNKS):
+        o_banks = [project(h_grp[0])]
+        h_grp.append(regroup_hidden(1))
+        for t in range(1, CHUNKS):
             if t + 1 < CHUNKS:
                 h_grp.append(regroup_hidden(t + 1))
             o_banks.append(project(h_grp[t]))
-            if t >= 1:
-                store(t - 1, o_banks[t - 1])
+            store(t - 1, o_banks[t - 1])
         store(CHUNKS - 1, o_banks[CHUNKS - 1])

@@ -20,6 +20,7 @@ CHUNK = 128
 CHUNKS = NODES // CHUNK
 PLANES_PER_BANK = 512 // CHUNK
 WARM_PASSES = 3
+W3_SCALAR = 128
 COUNT_COLS = 2
 HALF = DOUT // 2
 VECTOR_BANKS = ((2, 0), (2, 1), (3, 1))
@@ -185,7 +186,7 @@ def tile_perception_pb_s_kernel(tc, msg, adj, b2, W3, out):
         nc.tensor.transpose(b2_ps[:], b2_rows[:], ident_b[:])
         dd_banks += [outer_product(k) for k in range(1, CHUNKS)]
         w3_grp = keep.tile([P, DOUT, PACK], BF16, align_bytes=64)
-        regroup(nc.scalar.copy, w3_grp[:, 0 : DOUT // 2, :], w3_sb[:, :, 0 : DOUT // 2])
+        regroup(nc.scalar.copy, w3_grp[:, 0:W3_SCALAR, :], w3_sb[:, :, 0:W3_SCALAR])
         a_grp = [scaled(0, dd_banks[0])]
         b2_col = keep.tile([P, PACK], F32)
         h_planes = []
@@ -230,7 +231,7 @@ def tile_perception_pb_s_kernel(tc, msg, adj, b2, W3, out):
             regroup(nc.vector.tensor_copy, h_grp_t[:], h_planes[t][:])
             return h_grp_t
 
-        regroup(nc.vector.tensor_copy, w3_grp[:, DOUT // 2 : DOUT, :], w3_sb[:, :, DOUT // 2 : DOUT])
+        regroup(nc.vector.tensor_copy, w3_grp[:, W3_SCALAR:DOUT, :], w3_sb[:, :, W3_SCALAR:DOUT])
         h_grp = [regroup_hidden(0)]
         w3_codes, w3_scales = quantise(nc, keep, "w3", w3_grp)
         o_banks = [project(h_grp[0])]

@@ -19,7 +19,7 @@ DOUT = 512
 CHUNK = 128
 CHUNKS = NODES // CHUNK
 PLANES_PER_BANK = 512 // CHUNK
-WARM_PASSES = 3
+WARM_PASSES = 2
 W3_SCALAR = 128
 COUNT_COLS = 2
 HALF = DOUT // 2
@@ -85,8 +85,12 @@ def tile_perception_pb_s_kernel(tc, msg, adj, b2, W3, out):
         nc.scalar.activation(out=table_warm[:], in_=one_col[:], func=ACT.Abs_reciprocal_sqrt)
 
         warm_ps = psum.tile([P, P], F32, tag="bank")
-        for repeat in range(WARM_PASSES):
+
+        def warm_up():
             nc.tensor.matmul(out=warm_ps[:], lhsT=ident_f[:], rhs=ident_f[:], start=True, stop=True)
+
+        for repeat in range(WARM_PASSES):
+            warm_up()
 
         col_ps = psum.tile([P, 2, CHUNKS, COUNT_COLS], F32, tag="bank")
         row_ps = psum.tile([P, NODES], F32, tag="bank")
@@ -182,9 +186,12 @@ def tile_perception_pb_s_kernel(tc, msg, adj, b2, W3, out):
             return h_planes
 
         dd_banks = [outer_product(0)]
+        warm_up()
         b2_ps = psum.tile([P, P], BF16, tag="bank")
         nc.tensor.transpose(b2_ps[:], b2_rows[:], ident_b[:])
-        dd_banks += [outer_product(k) for k in range(1, CHUNKS)]
+        dd_banks.append(outer_product(1))
+        warm_up()
+        dd_banks += [outer_product(k) for k in range(2, CHUNKS)]
         w3_grp = keep.tile([P, DOUT, PACK], BF16, align_bytes=64)
         regroup(nc.scalar.copy, w3_grp[:, 0:W3_SCALAR, :], w3_sb[:, :, 0:W3_SCALAR])
         a_grp = [scaled(0, dd_banks[0])]

@@ -20,7 +20,7 @@ CHUNK = 128
 CHUNKS = NODES // CHUNK
 PLANES_PER_BANK = 512 // CHUNK
 WARM_PASSES = 2
-W3_SCALAR = 128
+W3_SCALAR = 192
 COUNT_COLS = 2
 HALF = DOUT // 2
 VECTOR_BANKS = ((2, 0), (2, 1), (3, 1))

from contextlib import ExitStack

import concourse.mybir as mybir
from concourse.masks import make_identity

F32 = mybir.dt.float32
BF16 = mybir.dt.bfloat16
U32 = mybir.dt.uint32
U8 = mybir.dt.uint8
FP8X4 = mybir.dt.float8_e4m3fn_x4
ALU = mybir.AluOpType
ACT = mybir.ActivationFunctionType

P = 128
PACK = 4
NODES = 512
HIDDEN = 512
DOUT = 512
CHUNK = 128
CHUNKS = NODES // CHUNK
PLANES_PER_BANK = 512 // CHUNK
WARM_PASSES = 2
W3_SCALAR = 192
COUNT_COLS = 2
HALF = DOUT // 2
VECTOR_BANKS = ((2, 0), (2, 1), (3, 1))

FLOPS = 2 * NODES * NODES * HIDDEN + 2 * NODES * HIDDEN * DOUT


def regroup(copy, grouped, planes):
    copy(
        out=grouped.rearrange("p (c i) q -> p c q i", i=4),
        in_=planes.rearrange("p q (c i) -> p c q i", i=4),
    )


def quantise(nc, pool, name, grouped):
    width = grouped.shape[1]
    codes = pool.tile([P, width], U32, name=name + "_codes", align_bytes=64)
    scales = pool.tile([P, width], U8, name=name + "_scales", align_bytes=64)
    nc.vector.quantize_mx(
        out=codes[:].bitcast(FP8X4),
        scales=scales[:],
        in_=grouped[:].rearrange("p w q -> p (w q)"),
    )
    return codes, scales


def tile_perception_pb_s_kernel(tc, msg, adj, b2, W3, out):
    nc = tc.nc
    with ExitStack() as ctx:
        ctx.enter_context(tc.manual_schedule())
        keep = ctx.enter_context(tc.tile_pool(name="keep", bufs=1))
        work = ctx.enter_context(tc.tile_pool(name="work", bufs=CHUNKS))
        psum = ctx.enter_context(tc.psum_pool(name="psum", bufs=8))

        adj_sb = keep.tile([P, PACK, NODES], BF16)
        for u in range(2):
            nc.sync.dma_start(
                out=adj_sb[:, 2 * u : 2 * u + 2, :],
                in_=adj[0, u * 2 * P : (u + 1) * 2 * P, :].rearrange("(p e) i -> p e i", e=2),
            )
        msg_sb = keep.tile([P, PACK, HIDDEN], BF16)
        for u in range(2):
            nc.sync.dma_start(
                out=msg_sb[:, 2 * u : 2 * u + 2, :],
                in_=msg[0, u * 2 * P : (u + 1) * 2 * P, :].rearrange("(p e) f -> p e f", e=2),
            )
        w3_sb = keep.tile([P, PACK, DOUT], BF16)
        nc.sync.dma_start(out=w3_sb[:], in_=W3.rearrange("(q p) o -> p q o", p=P))
        b2_rows = keep.tile([P, P], BF16)
        nc.vector.memset(b2_rows[:], 0.0)
        nc.scalar.dma_start(out=b2_rows[0:PACK, :], in_=b2.rearrange("(q p) -> q p", p=P))

        ones = keep.tile([P, P], BF16)
        nc.vector.memset(ones[:], 1.0)
        one_col = keep.tile([P, 1], F32)
        nc.vector.memset(one_col[:], 1.0)
        ident_f = keep.tile([P, P], F32)
        make_identity(nc, ident_f[:])
        ident_b = keep.tile([P, P], BF16)
        make_identity(nc, ident_b[:])
        table_warm = keep.tile([P, 1], F32)
        nc.scalar.activation(out=table_warm[:], in_=one_col[:], func=ACT.Abs_reciprocal_sqrt)

        warm_ps = psum.tile([P, P], F32, tag="bank")

        def warm_up():
            nc.tensor.matmul(out=warm_ps[:], lhsT=ident_f[:], rhs=ident_f[:], start=True, stop=True)

        for repeat in range(WARM_PASSES):
            warm_up()

        col_ps = psum.tile([P, 2, CHUNKS, COUNT_COLS], F32, tag="bank")
        row_ps = psum.tile([P, NODES], F32, tag="bank")
        pair_sums = []
        for pair in range(2):
            pair_sum = keep.tile([P, NODES], BF16, name="pair_sum%d" % pair)
            nc.vector.tensor_tensor(
                out=pair_sum[:], in0=adj_sb[:, 2 * pair, :], in1=adj_sb[:, 2 * pair + 1, :], op=ALU.add
            )
            pair_sums.append(pair_sum)

        def row_sums(pair):
            nc.tensor.matmul(out=row_ps[:], lhsT=ones[:], rhs=pair_sums[pair][:], start=(pair == 0), stop=(pair == 1))

        def column_sums(pair):
            for k in range(CHUNKS):
                nc.tensor.matmul(
                    out=col_ps[:, pair, k, :],
                    lhsT=pair_sums[pair][:, k * CHUNK : (k + 1) * CHUNK],
                    rhs=ones[:, 0:COUNT_COLS],
                    start=True,
                    stop=True,
                )

        row_sums(0)
        column_sums(0)
        column_sums(1)
        row_sums(1)

        adj_grp = keep.tile([P, NODES, PACK], BF16, align_bytes=64)

        def regroup_adj(copy, k):
            cols = slice(k * CHUNK, (k + 1) * CHUNK)
            regroup(copy, adj_grp[:, cols, :], adj_sb[:, :, cols])

        for k in range(2, CHUNKS):
            regroup_adj(nc.scalar.copy, k)
        for k in range(2):
            regroup_adj(nc.vector.tensor_copy, k)
        c_col = keep.tile([P, CHUNKS], F32)
        nc.vector.tensor_reduce(
            out=c_col[:], in_=col_ps[:, :, :, 0].rearrange("p s k -> p k s"), axis=mybir.AxisListType.X, op=ALU.add
        )

        msg_halves = [slice(0, HIDDEN // 2), slice(HIDDEN // 2, HIDDEN)]
        msg_grp = [keep.tile([P, HIDDEN // 2, PACK], BF16, name="msg_grp%d" % m, align_bytes=64) for m in range(2)]
        for m in range(2):
            regroup(nc.vector.tensor_copy, msg_grp[m][:], msg_sb[:, :, msg_halves[m]])
        msg_words = [quantise(nc, keep, "msg%d" % m, msg_grp[m]) for m in range(2)]

        def outer_product(k):
            dd = work.tile([P, NODES], BF16, name="dd")
            nc.scalar.activation(out=dd[:], in_=row_ps[:], func=ACT.Abs_reciprocal_sqrt, scale=c_col[:, k : k + 1])
            dd_ps = psum.tile([P, 2, CHUNK], F32, name="dd_ps", tag="bank")
            words = dd[:].bitcast(F32)
            for u in range(2):
                nc.tensor.transpose(dd_ps[:, u, :], words[:, u * P : (u + 1) * P], ident_f[:])
            return dd_ps

        def scaled(k, dd_ps):
            a_grp = work.tile([P, CHUNK, PACK], BF16, name="a_grp", align_bytes=64)
            nc.vector.tensor_tensor(
                out=a_grp[:].rearrange("p n (u e) -> p n u e", e=2),
                in0=adj_grp[:, k * CHUNK : (k + 1) * CHUNK, :].rearrange("p n (u e) -> p n u e", e=2),
                in1=dd_ps[:].bitcast(BF16).rearrange("p u (n e) -> p n u e", e=2),
                op=ALU.mult,
            )
            return a_grp

        def hidden(a_grp):
            a_codes, a_scales = quantise(nc, work, "a", a_grp)
            h_planes = work.tile([P, PACK, CHUNK], BF16, name="h_planes")
            for b in range(PACK // PLANES_PER_BANK):
                h_ps = psum.tile([P, PLANES_PER_BANK, CHUNK], F32, name="h_ps", tag="bank")
                for r in range(PLANES_PER_BANK):
                    q = b * PLANES_PER_BANK + r
                    msg_codes, msg_scales = msg_words[q // 2]
                    features = slice(q % 2 * P, (q % 2 + 1) * P)
                    nc.tensor.matmul_mx(
                        out=h_ps[:, r, :],
                        lhsT=msg_codes[:, features].bitcast(FP8X4),
                        lhsT_scale=msg_scales[:, features],
                        rhs=a_codes[:].bitcast(FP8X4),
                        rhs_scale=a_scales[:],
                        start=True,
                        stop=True,
                    )
                for r in range(PLANES_PER_BANK):
                    q = b * PLANES_PER_BANK + r
                    nc.scalar.activation(
                        out=h_planes[:, q, :], in_=h_ps[:, r, :], func=ACT.Relu, bias=b2_col[:, q : q + 1]
                    )
            return h_planes

        dd_banks = [outer_product(0)]
        warm_up()
        b2_ps = psum.tile([P, P], BF16, tag="bank")
        nc.tensor.transpose(b2_ps[:], b2_rows[:], ident_b[:])
        dd_banks.append(outer_product(1))
        warm_up()
        dd_banks += [outer_product(k) for k in range(2, CHUNKS)]
        w3_grp = keep.tile([P, DOUT, PACK], BF16, align_bytes=64)
        regroup(nc.scalar.copy, w3_grp[:, 0:W3_SCALAR, :], w3_sb[:, :, 0:W3_SCALAR])
        a_grp = [scaled(0, dd_banks[0])]
        b2_col = keep.tile([P, PACK], F32)
        h_planes = []
        for t in range(CHUNKS):
            if t + 1 < CHUNKS:
                a_grp.append(scaled(t + 1, dd_banks[t + 1]))
            if t == 0:
                nc.vector.tensor_copy(out=b2_col[:], in_=b2_ps[:, 0:PACK])
            h_planes.append(hidden(a_grp[t]))

        def project(h_grp_t):
            h_codes, h_scales = quantise(nc, work, "h", h_grp_t)
            banks = []
            for half in range(2):
                o_cols = slice(half * HALF, (half + 1) * HALF)
                o_ps = psum.tile([P, HALF], F32, name="o_ps", tag="bank")
                nc.tensor.matmul_mx(
                    out=o_ps[:],
                    lhsT=h_codes[:].bitcast(FP8X4),
                    lhsT_scale=h_scales[:],
                    rhs=w3_codes[:, o_cols].bitcast(FP8X4),
                    rhs_scale=w3_scales[:, o_cols],
                    start=True,
                    stop=True,
                )
                banks.append(o_ps)
            return banks

        def store(t, banks):
            for half in range(2):
                o_sb = work.tile([P, HALF], F32, name="o_sb", bufs=2 * CHUNKS)
                if (t, half) in VECTOR_BANKS:
                    nc.vector.tensor_copy(out=o_sb[:], in_=banks[half][:])
                else:
                    nc.scalar.copy(out=o_sb[:], in_=banks[half][:])
                nc.sync.dma_start(
                    out=out[0, t * CHUNK : (t + 1) * CHUNK, half * HALF : (half + 1) * HALF], in_=o_sb[:]
                )

        def regroup_hidden(t):
            h_grp_t = work.tile([P, CHUNK, PACK], BF16, name="h_grp", align_bytes=64)
            regroup(nc.vector.tensor_copy, h_grp_t[:], h_planes[t][:])
            return h_grp_t

        regroup(nc.vector.tensor_copy, w3_grp[:, W3_SCALAR:DOUT, :], w3_sb[:, :, W3_SCALAR:DOUT])
        h_grp = [regroup_hidden(0)]
        w3_codes, w3_scales = quantise(nc, keep, "w3", w3_grp)
        o_banks = [project(h_grp[0])]
        h_grp.append(regroup_hidden(1))
        for t in range(1, CHUNKS):
            if t + 1 < CHUNKS:
                h_grp.append(regroup_hidden(t + 1))
            o_banks.append(project(h_grp[t]))
            store(t - 1, o_banks[t - 1])
        store(CHUNKS - 1, o_banks[CHUNKS - 1])
